import numpy as np
import ml_dtypes


BF16 = ml_dtypes.bfloat16


def bf(x):
    return np.asarray(x, np.float32).astype(BF16)


def f64(x):
    return np.asarray(x).astype(np.float64)


E2M1 = np.array([0.0, 0.5, 1.0, 1.5, 2.0, 3.0, 4.0, 6.0, -0.0, -0.5, -1.0, -1.5, -2.0, -3.0, -4.0, -6.0])


def pack_weight(w, fmt):
    k, n = w.shape
    w = f64(bf(w)).reshape(k // 32, 32, n)
    amax = np.abs(w).max(1)
    if fmt == "e4m3":
        byte = np.frexp(amax)[1] - 1 + 127 - 7
    else:
        mant, ex = np.frexp(amax / 6.0)
        byte = np.where(mant > 0.5, ex, ex - 1) + 127
    byte = np.clip(np.where(amax > 0, byte, 1), 1, 254)
    scaled = (w * np.exp2(127.0 - byte)[:, None, :]).reshape(k, n).astype(np.float32)
    by_word = np.ascontiguousarray(scaled.reshape(k // 512, 128, 4, n).transpose(0, 1, 3, 2))
    if fmt == "e4m3":
        words = by_word.astype(ml_dtypes.float8_e4m3fn).view(np.uint8)
    else:
        c = by_word.astype(ml_dtypes.float4_e2m1fn).view(np.uint8) & 0xF
        words = c[..., 0::2] | (c[..., 1::2] << 4)
    return np.ascontiguousarray(words), np.ascontiguousarray(byte.astype(np.uint8).reshape(k // 512, 16, n))


def unpack_weight(words, scales, fmt):
    g, p, n, _ = words.shape
    if fmt == "e4m3":
        vals = np.ascontiguousarray(words).view(ml_dtypes.float8_e4m3fn).astype(np.float64)
    else:
        nib = np.empty((g, p, n, 4), np.uint8)
        nib[..., 0::2] = words & 0xF
        nib[..., 1::2] = words >> 4
        vals = E2M1[nib]
    vals = vals * np.repeat(np.exp2(scales.astype(np.float64) - 127.0), 8, axis=1)[..., None]
    return vals.transpose(0, 1, 3, 2).reshape(g * 512, n)

def pack4(w):
    words, scales = pack_weight(w, "e2m1")
    return words.reshape(words.shape[0], 128, -1), scales


def unpack4(words, scales):
    return unpack_weight(words.reshape(words.shape[0], 128, -1, 2), scales, "e2m1")


def kspread(k):
    return np.exp2(np.repeat(np.random.randint(-6, 7, k // 32), 32).astype(np.float64))


B, L, K, D, H = 4, 128, 4096, 512, 2
DH = D // H
RD = D // 2
HALF = RD // 2
ROPE_BASE = 10000.0


def apply_rope(t):
    pos = np.arange(L, dtype=np.float64)[:, None]
    inv = np.exp(np.arange(0, RD, 2, dtype=np.float64) * (-np.log(ROPE_BASE) / RD))
    theta = pos * inv
    cos, sin = np.cos(theta), np.sin(theta)
    t1, t2 = t[..., :HALF], t[..., HALF:RD]
    return np.concatenate([t1 * cos - t2 * sin, t1 * sin + t2 * cos], axis=-1)


def split_heads(t):
    return t.reshape(B, L, H, DH).transpose(0, 2, 1, 3)


def setup_inputs():
    s = kspread(K)
    x = np.random.standard_normal((B, L, K)) * s
    x_words, x_scales = pack4(np.ascontiguousarray(x.reshape(B * L, K).T))
    w = np.random.standard_normal((3 * D, K)) / np.sqrt(K) / s[None, :]
    words, scales = pack4(np.ascontiguousarray(w.T))
    b = bf(np.random.standard_normal(3 * D) * 0.3)
    return {"x_words": x_words,
            "x_scales": x_scales,
            "Wqkv_w_words": words,
            "Wqkv_w_scales": scales,
            "Wqkv_b": b}


def reference(x_words, x_scales, Wqkv_w_words, Wqkv_w_scales, Wqkv_b):
    xq = unpack4(x_words, x_scales).T.reshape(B, L, K)
    qkv = (xq @ unpack4(Wqkv_w_words, Wqkv_w_scales)) + f64(Wqkv_b)
    q, k, v = np.split(qkv, 3, axis=-1)
    q, k, v = split_heads(q), split_heads(k), split_heads(v)
    return apply_rope(q), apply_rope(k), v

@@ -1,0 +1,267 @@
+from contextlib import ExitStack
+import math
+
+import concourse.mybir as mybir
+
+FLOPS = 2 * 512 * 4096 * 1536
+
+F32 = mybir.dt.float32
+BF16 = mybir.dt.bfloat16
+I32 = mybir.dt.int32
+U8 = mybir.dt.uint8
+FP4X4 = mybir.dt.float4_e2m1fn_x4
+ALU = mybir.AluOpType
+FN = mybir.ActivationFunctionType
+
+P = 128
+PASSES = 8
+TILES = 4
+NBLK = 512
+HALF = 128
+ROPE_BASE = 10000.0
+
+SPLIT = 4
+NDUMMY = 3
+
+TWO_PI_HI = 6.28125
+TWO_PI_LO = 2.0 * math.pi - TWO_PI_HI
+
+
+def tile_ropeattention_pa_kernel(tc, x_words, x_scales, w_words, w_scales, bias, out_q, out_k, out_v):
+    nc = tc.nc
+    outs = [out_q, out_k, out_v]
+
+    with ExitStack() as ctx:
+        keep = ctx.enter_context(tc.tile_pool(name="keep", bufs=1))
+        work = ctx.enter_context(tc.tile_pool(name="work", bufs=4))
+        psum = ctx.enter_context(tc.psum_pool(name="psum", bufs=8))
+        ctx.enter_context(tc.manual_schedule())
+
+        def byte_tile(name, n_pass, n_bytes):
+            return keep.tile([P, n_pass, n_bytes], U8, name=name, align_bytes=64)
+
+        x_code_runs = [(0, 1), (1, 3), (4, 4)]
+        wq_code_runs = [(0, 1), (1, 3), (4, 4)]
+        w_code_runs = [(0, 4), (4, 4)]
+        first_scale_runs = [(0, 4), (4, 4)]
+        late_scale_runs = [(0, 8)]
+
+        xc = [byte_tile("xc%d" % i, n, 2 * 512) for i, (g0, n) in enumerate(x_code_runs)]
+        wc = [
+            [byte_tile("wc0_%d" % i, n, 2 * NBLK) for i, (g0, n) in enumerate(wq_code_runs)],
+            [byte_tile("wc1_%d" % i, n, 2 * NBLK) for i, (g0, n) in enumerate(w_code_runs)],
+            [byte_tile("wc2_%d" % i, n, 2 * NBLK) for i, (g0, n) in enumerate(w_code_runs)],
+        ]
+        wc_runs = [wq_code_runs, w_code_runs, w_code_runs]
+        xs = [byte_tile("xs%d" % i, n, 512) for i, (g0, n) in enumerate(first_scale_runs)]
+        ws = [
+            [byte_tile("ws0_%d" % i, n, NBLK) for i, (g0, n) in enumerate(first_scale_runs)],
+            [byte_tile("ws1_%d" % i, n, NBLK) for i, (g0, n) in enumerate(late_scale_runs)],
+            [byte_tile("ws2_%d" % i, n, NBLK) for i, (g0, n) in enumerate(late_scale_runs)],
+        ]
+        ws_runs = [first_scale_runs, late_scale_runs, late_scale_runs]
+
+        def find(runs, tiles, g):
+            for (g0, n), t in zip(runs, tiles):
+                if g0 <= g < g0 + n:
+                    return t, g - g0
+            raise ValueError("pass not loaded")
+
+        brow = keep.tile([P, 3 * NBLK], BF16, name="brow")
+        ones = keep.tile([P, P], BF16, name="ones")
+        junk = keep.tile([P, NBLK], BF16, name="junk")
+        bias_v = keep.tile([P, NBLK], F32, name="bias_v")
+        seed = keep.tile([P, 1], F32, name="seed")
+        seed2 = keep.tile([P, 1], F32, name="seed2")
+        pos = keep.tile([P, 1], F32, name="pos")
+        inv = keep.tile([P, HALF], F32, name="inv")
+        phi = keep.tile([P, 3 * HALF], F32, name="phi")
+        turns = keep.tile([P, 3 * HALF], I32, name="turns")
+        red1 = keep.tile([P, 3 * HALF], F32, name="red1")
+        red2 = keep.tile([P, 3 * HALF], F32, name="red2")
+        shalf = keep.tile([P, 3 * HALF], F32, name="shalf")
+        sq = keep.tile([P, 3 * HALF], F32, name="sq")
+        trig = keep.tile([P, 3, HALF], F32, name="trig")
+        rotb = [keep.tile([P, NBLK], F32, name="rotb%d" % b) for b in range(2)]
+
+        nc.gpsimd.memset(junk[:], 0.0)
+        nc.gpsimd.memset(ones[:], 1.0)
+        nc.gpsimd.memset(seed[:], 0.0)
+        nc.gpsimd.iota(pos[:], pattern=[[0, 1]], base=0, channel_multiplier=1, allow_small_or_imprecise_dtypes=True)
+        nc.gpsimd.memset(inv[:, 0:1], 1.0)
+        ratio = ROPE_BASE ** (-1.0 / HALF)
+        for k in range(7):
+            w = 1 << k
+            nc.gpsimd.tensor_scalar(
+                out=inv[:, w : 2 * w], in0=inv[:, 0:w], scalar1=ratio**w, scalar2=0.0, op0=ALU.mult, op1=ALU.add
+            )
+        for i, shift in enumerate((0.0, 0.5 * math.pi, -0.5 * math.pi)):
+            nc.gpsimd.tensor_scalar(
+                out=phi[:, HALF * i : HALF * (i + 1)], in0=inv[:], scalar1=pos[:, 0:1], scalar2=shift, op0=ALU.mult, op1=ALU.add
+            )
+
+        nc.vector.memset(brow[:].bitcast(I32), 0)
+        nc.vector.memset(xs[0][:].bitcast(I32), 0)
+        nc.vector.memset(ws[0][0][:].bitcast(I32), 0)
+        nc.vector.memset(xs[1][:].bitcast(I32), 0)
+        nc.vector.memset(ws[0][1][:].bitcast(I32), 0)
+        nc.vector.memset(ws[1][0][:].bitcast(I32), 0)
+        nc.vector.memset(ws[2][0][:].bitcast(I32), 0)
+
+        nc.scalar.dma_start(out=brow[0:1, :], in_=bias.rearrange("(o n) -> o n", o=1))
+        nc.scalar.activation(out=seed2[:], in_=seed[:], func=FN.Sin)
+
+        def load_codes(t, words, g0, n, c0, c1):
+            nc.sync.dma_start(
+                out=t[:].bitcast(I32),
+                in_=words[g0 : g0 + n, :, c0:c1].rearrange("g p n -> p g n").bitcast(I32),
+            )
+
+        def load_scales(t, scales, g0, n, c0, c1):
+            for q in range(4):
+                nc.sync.dma_start(
+                    out=t[32 * q : 32 * q + 4, :, :].bitcast(I32),
+                    in_=scales[g0 : g0 + n, 4 * q : 4 * q + 4, c0:c1].rearrange("g r n -> r g n").bitcast(I32),
+                )
+
+        def load_x_codes(i):
+            load_codes(xc[i], x_words, x_code_runs[i][0], x_code_runs[i][1], 0, 1024)
+
+        def load_w_codes(b, i):
+            load_codes(wc[b][i], w_words, wc_runs[b][i][0], wc_runs[b][i][1], 1024 * b, 1024 * (b + 1))
+
+        def load_x_scales(i):
+            load_scales(xs[i], x_scales, first_scale_runs[i][0], first_scale_runs[i][1], 0, 512)
+
+        def load_w_scales(b, i):
+            load_scales(ws[b][i], w_scales, ws_runs[b][i][0], ws_runs[b][i][1], NBLK * b, NBLK * (b + 1))
+
+        load_x_codes(0)
+        load_w_codes(0, 0)
+        load_x_scales(0)
+        load_w_scales(0, 0)
+        load_x_codes(1)
+        load_w_codes(0, 1)
+        load_x_scales(1)
+        load_w_scales(0, 1)
+        load_x_codes(2)
+        load_w_codes(0, 2)
+        load_w_scales(1, 0)
+        load_w_codes(1, 0)
+        load_w_codes(1, 1)
+        load_w_scales(2, 0)
+        load_w_codes(2, 0)
+        load_w_codes(2, 1)
+
+        warm = psum.tile([P, NBLK], F32, name="warm", tag="acc")
+        for i in range(NDUMMY):
+            nc.tensor.matmul(out=warm[:], lhsT=junk[:, 0:P], rhs=junk[:], start=True, stop=True)
+        bp = []
+        for b in range(3):
+            bpt = psum.tile([P, NBLK], F32, name="bp%d" % b, tag="acc")
+            nc.tensor.matmul(out=bpt[:], lhsT=ones[:], rhs=brow[:, NBLK * b : NBLK * (b + 1)], start=True, stop=True)
+            bp.append(bpt)
+
+        nc.vector.tensor_scalar(out=turns[:], in0=phi[:], scalar1=1.0 / (2.0 * math.pi), scalar2=None, op0=ALU.mult)
+        nc.vector.scalar_tensor_tensor(out=red1[:], in0=turns[:], scalar=-TWO_PI_HI, in1=phi[:], op0=ALU.mult, op1=ALU.add)
+        nc.vector.scalar_tensor_tensor(out=red2[:], in0=turns[:], scalar=-TWO_PI_LO, in1=red1[:], op0=ALU.mult, op1=ALU.add)
+        nc.scalar.activation(out=shalf[:], in_=red2[:], func=FN.Sin, scale=0.5)
+        nc.scalar.activation(out=sq[:], in_=shalf[:], func=FN.Square)
+        nc.scalar.activation(out=trig[:].rearrange("p a j -> p (a j)"), in_=sq[:], func=FN.Copy, scale=-2.0, bias=1.0)
+        nc.scalar.copy(out=bias_v[:], in_=bp[2][:])
+
+        cos_b = trig[:, 0:1, :].to_broadcast([P, 4, HALF])
+        sin_b = trig[:, 1:3, :].unsqueeze(1).to_broadcast([P, 2, 2, HALF])
+
+        def rotate_products(src):
+            pc = work.tile([P, NBLK], F32, name="pc")
+            nc.vector.tensor_tensor(
+                out=pc[:].rearrange("p (a j) -> p a j", a=4), in0=src.rearrange("p (a j) -> p a j", a=4), in1=cos_b, op=ALU.mult
+            )
+            qs = work.tile([P, NBLK], F32, name="qs")
+            nc.vector.tensor_tensor(
+                out=qs[:].rearrange("p (h s j) -> p h s j", h=2, s=2),
+                in0=src.rearrange("p (h s j) -> p h s j", h=2, s=2)[:, :, ::-1, :],
+                in1=sin_b,
+                op=ALU.mult,
+            )
+            return pc, qs
+
+        for b in range(2):
+            pc, qs = rotate_products(bp[b][:])
+            nc.gpsimd.tensor_tensor(out=rotb[b][:], in0=pc[:], in1=qs[:], op=ALU.add)
+
+        def mx_pass(acc, t, b, g, c0, c1):
+            xct, xi = find(x_code_runs, xc, g)
+            xst, xj = find(first_scale_runs, xs, g)
+            wct, wi = find(wc_runs[b], wc[b], g)
+            wst, wj = find(ws_runs[b], ws[b], g)
+            nc.tensor.matmul_mx(
+                out=acc[:],
+                lhsT=xct[:, xi, 256 * t : 256 * (t + 1)].bitcast(FP4X4),
+                lhsT_scale=xst[:, xj, P * t : P * (t + 1)],
+                rhs=wct[:, wi, 2 * c0 : 2 * c1].bitcast(FP4X4),
+                rhs_scale=wst[:, wj, c0:c1],
+                start=(g == 0),
+                stop=(g == PASSES - 1),
+            )
+
+        pending = []
+
+        def finish_pending():
+            for (b, t, pc, qs) in pending:
+                nc.vector.tensor_tensor(out=pc[:], in0=pc[:], in1=qs[:], op=ALU.add)
+                res = work.tile([P, NBLK], F32, name="res")
+                nc.gpsimd.tensor_tensor(out=res[:], in0=pc[:], in1=rotb[b][:], op=ALU.add)
+                nc.sync.dma_start(out=outs[b][t].rearrange("h l d -> l h d"), in_=res[:].rearrange("p (h d) -> p h d", h=2))
+            pending.clear()
+
+        def rope_epilogue(acc, b, t):
+            src = acc[:]
+            pc = work.tile([P, NBLK], F32, name="pc")
+            nc.vector.tensor_tensor(
+                out=pc[:].rearrange("p (a j) -> p a j", a=4), in0=src.rearrange("p (a j) -> p a j", a=4), in1=cos_b, op=ALU.mult
+            )
+            finish_pending()
+            qs = work.tile([P, NBLK], F32, name="qs")
+            nc.vector.tensor_tensor(
+                out=qs[:].rearrange("p (h s j) -> p h s j", h=2, s=2),
+                in0=src.rearrange("p (h s j) -> p h s j", h=2, s=2)[:, :, ::-1, :],
+                in1=sin_b,
+                op=ALU.mult,
+            )
+            pending.append((b, t, pc, qs))
+
+        accs = []
+        for t in range(TILES):
+            acc = psum.tile([P, NBLK], F32, name="acc", tag="acc")
+            accs.append(acc)
+        for g in range(SPLIT):
+            for t in range(TILES):
+                mx_pass(accs[t], t, 0, g, 0, NBLK)
+        for t in range(TILES):
+            for g in range(SPLIT, PASSES):
+                mx_pass(accs[t], t, 0, g, 0, NBLK)
+            rope_epilogue(accs[t], 0, t)
+        for t in range(TILES):
+            acc = psum.tile([P, NBLK], F32, name="acc", tag="acc")
+            for g in range(PASSES):
+                mx_pass(acc, t, 1, g, 0, NBLK)
+            rope_epilogue(acc, 1, t)
+        for t in range(TILES - 1):
+            acc = psum.tile([P, NBLK], F32, name="acc", tag="acc")
+            for g in range(PASSES):
+                mx_pass(acc, t, 2, g, 0, NBLK)
+            resv = work.tile([P, NBLK], F32, name="resv")
+            nc.vector.tensor_tensor(out=resv[:], in0=acc[:], in1=bias_v[:], op=ALU.add)
+            finish_pending()
+            nc.scalar.dma_start(out=out_v[t].rearrange("h l d -> l h d"), in_=resv[:].rearrange("p (h d) -> p h d", h=2))
+        t = TILES - 1
+        for h in range(2):
+            acc = psum.tile([P, NBLK // 2], F32, name="acch", tag="acc")
+            for g in range(PASSES):
+                mx_pass(acc, t, 2, g, 256 * h, 256 * (h + 1))
+            resh = work.tile([P, NBLK // 2], F32, name="resh")
+            nc.vector.tensor_tensor(out=resh[:], in0=acc[:], in1=bias_v[:, 256 * h : 256 * (h + 1)], op=ALU.add)
+            eng = nc.scalar if h == 0 else nc.sync
+            eng.dma_start(out=out_v[t][h], in_=resh[:])

@@ -20,8 +20,9 @@ NBLK = 512
 HALF = 128
 ROPE_BASE = 10000.0
 
-SPLIT = 4
-NDUMMY = 3
+SPLIT_Q = 8
+SPLIT_K = 4
+NDUMMY = 16
 
 TWO_PI_HI = 6.28125
 TWO_PI_LO = 2.0 * math.pi - TWO_PI_HI
@@ -40,8 +41,8 @@ def tile_ropeattention_pa_kernel(tc, x_words, x_scales, w_words, w_scales, bias,
         def byte_tile(name, n_pass, n_bytes):
             return keep.tile([P, n_pass, n_bytes], U8, name=name, align_bytes=64)
 
-        x_code_runs = [(0, 1), (1, 3), (4, 4)]
-        wq_code_runs = [(0, 1), (1, 3), (4, 4)]
+        x_code_runs = [(0, 1), (1, 3), (4, 2), (6, 2)]
+        wq_code_runs = [(0, 1), (1, 3), (4, 2), (6, 2)]
         w_code_runs = [(0, 4), (4, 4)]
         first_scale_runs = [(0, 4), (4, 4)]
         late_scale_runs = [(0, 8)]
@@ -69,7 +70,6 @@ def tile_ropeattention_pa_kernel(tc, x_words, x_scales, w_words, w_scales, bias,
 
         brow = keep.tile([P, 3 * NBLK], BF16, name="brow")
         ones = keep.tile([P, P], BF16, name="ones")
-        junk = keep.tile([P, NBLK], BF16, name="junk")
         bias_v = keep.tile([P, NBLK], F32, name="bias_v")
         seed = keep.tile([P, 1], F32, name="seed")
         seed2 = keep.tile([P, 1], F32, name="seed2")
@@ -84,7 +84,6 @@ def tile_ropeattention_pa_kernel(tc, x_words, x_scales, w_words, w_scales, bias,
         trig = keep.tile([P, 3, HALF], F32, name="trig")
         rotb = [keep.tile([P, NBLK], F32, name="rotb%d" % b) for b in range(2)]
 
-        nc.gpsimd.memset(junk[:], 0.0)
         nc.gpsimd.memset(ones[:], 1.0)
         nc.gpsimd.memset(seed[:], 0.0)
         nc.gpsimd.iota(pos[:], pattern=[[0, 1]], base=0, channel_multiplier=1, allow_small_or_imprecise_dtypes=True)
@@ -146,6 +145,8 @@ def tile_ropeattention_pa_kernel(tc, x_words, x_scales, w_words, w_scales, bias,
         load_w_scales(0, 1)
         load_x_codes(2)
         load_w_codes(0, 2)
+        load_x_codes(3)
+        load_w_codes(0, 3)
         load_w_scales(1, 0)
         load_w_codes(1, 0)
         load_w_codes(1, 1)
@@ -155,7 +156,7 @@ def tile_ropeattention_pa_kernel(tc, x_words, x_scales, w_words, w_scales, bias,
 
         warm = psum.tile([P, NBLK], F32, name="warm", tag="acc")
         for i in range(NDUMMY):
-            nc.tensor.matmul(out=warm[:], lhsT=junk[:, 0:P], rhs=junk[:], start=True, stop=True)
+            nc.tensor.matmul(out=warm[:, 0:P], lhsT=ones[:], rhs=ones[:], start=True, stop=True)
         bp = []
         for b in range(3):
             bpt = psum.tile([P, NBLK], F32, name="bp%d" % b, tag="acc")
@@ -236,18 +237,24 @@ def tile_ropeattention_pa_kernel(tc, x_words, x_scales, w_words, w_scales, bias,
         for t in range(TILES):
             acc = psum.tile([P, NBLK], F32, name="acc", tag="acc")
             accs.append(acc)
-        for g in range(SPLIT):
+        for g in range(SPLIT_Q):
             for t in range(TILES):
                 mx_pass(accs[t], t, 0, g, 0, NBLK)
         for t in range(TILES):
-            for g in range(SPLIT, PASSES):
+            for g in range(SPLIT_Q, PASSES):
                 mx_pass(accs[t], t, 0, g, 0, NBLK)
             rope_epilogue(accs[t], 0, t)
+        accs = []
         for t in range(TILES):
             acc = psum.tile([P, NBLK], F32, name="acc", tag="acc")
-            for g in range(PASSES):
-                mx_pass(acc, t, 1, g, 0, NBLK)
-            rope_epilogue(acc, 1, t)
+            accs.append(acc)
+        for g in range(SPLIT_K):
+            for t in range(TILES):
+                mx_pass(accs[t], t, 1, g, 0, NBLK)
+        for t in range(TILES):
+            for g in range(SPLIT_K, PASSES):
+                mx_pass(accs[t], t, 1, g, 0, NBLK)
+            rope_epilogue(accs[t], 1, t)
         for t in range(TILES - 1):
             acc = psum.tile([P, NBLK], F32, name="acc", tag="acc")
             for g in range(PASSES):

@@ -22,7 +22,8 @@ ROPE_BASE = 10000.0
 
 SPLIT_Q = 8
 SPLIT_K = 4
-NDUMMY = 16
+NDUMMY = 24
+NBRIDGE = 6
 
 TWO_PI_HI = 6.28125
 TWO_PI_LO = 2.0 * math.pi - TWO_PI_HI
@@ -162,6 +163,8 @@ def tile_ropeattention_pa_kernel(tc, x_words, x_scales, w_words, w_scales, bias,
             bpt = psum.tile([P, NBLK], F32, name="bp%d" % b, tag="acc")
             nc.tensor.matmul(out=bpt[:], lhsT=ones[:], rhs=brow[:, NBLK * b : NBLK * (b + 1)], start=True, stop=True)
             bp.append(bpt)
+        for i in range(NBRIDGE):
+            nc.tensor.matmul(out=warm[:], lhsT=ones[:], rhs=brow[:, 0:NBLK], start=True, stop=True)
 
         nc.vector.tensor_scalar(out=turns[:], in0=phi[:], scalar1=1.0 / (2.0 * math.pi), scalar2=None, op0=ALU.mult)
         nc.vector.scalar_tensor_tensor(out=red1[:], in0=turns[:], scalar=-TWO_PI_HI, in1=phi[:], op0=ALU.mult, op1=ALU.add)

@@ -15,18 +15,24 @@ FN = mybir.ActivationFunctionType
 
 P = 128
 PASSES = 8
-TILES = 4
-NBLK = 512
+BATCHES = 4
+BLOCK = 512
+HEADS = 2
 HALF = 128
 ROPE_BASE = 10000.0
-
-SPLIT_Q = 8
-SPLIT_K = 4
-NDUMMY = 24
-NBRIDGE = 6
+Q_BLOCK = 0
+K_BLOCK = 1
+V_BLOCK = 2
 
 TWO_PI_HI = 6.28125
 TWO_PI_LO = 2.0 * math.pi - TWO_PI_HI
+
+EARLY_CODE_LOADS = [(0, 1), (1, 3), (4, 2), (6, 2)]
+LATE_CODE_LOADS = [(0, 4), (4, 4)]
+EARLY_SCALE_LOADS = [(0, 4), (4, 4)]
+LATE_SCALE_LOADS = [(0, 8)]
+
+PASS_OUTER = {Q_BLOCK: 8, K_BLOCK: 4}
 
 
 def tile_ropeattention_pa_kernel(tc, x_words, x_scales, w_words, w_scales, bias, out_q, out_k, out_v):
@@ -39,239 +45,223 @@ def tile_ropeattention_pa_kernel(tc, x_words, x_scales, w_words, w_scales, bias,
         psum = ctx.enter_context(tc.psum_pool(name="psum", bufs=8))
         ctx.enter_context(tc.manual_schedule())
 
-        def byte_tile(name, n_pass, n_bytes):
-            return keep.tile([P, n_pass, n_bytes], U8, name=name, align_bytes=64)
+        def byte_tiles(name, loads, row_bytes):
+            return [
+                keep.tile([P, n, row_bytes], U8, name="%s_%d" % (name, i), align_bytes=64)
+                for i, (first, n) in enumerate(loads)
+            ]
 
-        x_code_runs = [(0, 1), (1, 3), (4, 2), (6, 2)]
-        wq_code_runs = [(0, 1), (1, 3), (4, 2), (6, 2)]
-        w_code_runs = [(0, 4), (4, 4)]
-        first_scale_runs = [(0, 4), (4, 4)]
-        late_scale_runs = [(0, 8)]
+        w_code_loads = [EARLY_CODE_LOADS, LATE_CODE_LOADS, LATE_CODE_LOADS]
+        w_scale_loads = [EARLY_SCALE_LOADS, LATE_SCALE_LOADS, LATE_SCALE_LOADS]
+        x_codes = byte_tiles("x_codes", EARLY_CODE_LOADS, 2 * BATCHES * P)
+        x_planes = byte_tiles("x_planes", EARLY_SCALE_LOADS, BATCHES * P)
+        w_codes = [byte_tiles("w_codes%d" % b, w_code_loads[b], 2 * BLOCK) for b in range(3)]
+        w_planes = [byte_tiles("w_planes%d" % b, w_scale_loads[b], BLOCK) for b in range(3)]
 
-        xc = [byte_tile("xc%d" % i, n, 2 * 512) for i, (g0, n) in enumerate(x_code_runs)]
-        wc = [
-            [byte_tile("wc0_%d" % i, n, 2 * NBLK) for i, (g0, n) in enumerate(wq_code_runs)],
-            [byte_tile("wc1_%d" % i, n, 2 * NBLK) for i, (g0, n) in enumerate(w_code_runs)],
-            [byte_tile("wc2_%d" % i, n, 2 * NBLK) for i, (g0, n) in enumerate(w_code_runs)],
-        ]
-        wc_runs = [wq_code_runs, w_code_runs, w_code_runs]
-        xs = [byte_tile("xs%d" % i, n, 512) for i, (g0, n) in enumerate(first_scale_runs)]
-        ws = [
-            [byte_tile("ws0_%d" % i, n, NBLK) for i, (g0, n) in enumerate(first_scale_runs)],
-            [byte_tile("ws1_%d" % i, n, NBLK) for i, (g0, n) in enumerate(late_scale_runs)],
-            [byte_tile("ws2_%d" % i, n, NBLK) for i, (g0, n) in enumerate(late_scale_runs)],
-        ]
-        ws_runs = [first_scale_runs, late_scale_runs, late_scale_runs]
-
-        def find(runs, tiles, g):
-            for (g0, n), t in zip(runs, tiles):
-                if g0 <= g < g0 + n:
-                    return t, g - g0
+        def of_pass(loads, tiles, g):
+            for (first, n), t in zip(loads, tiles):
+                if first <= g < first + n:
+                    return t[:, g - first, :]
             raise ValueError("pass not loaded")
 
-        brow = keep.tile([P, 3 * NBLK], BF16, name="brow")
-        ones = keep.tile([P, P], BF16, name="ones")
-        bias_v = keep.tile([P, NBLK], F32, name="bias_v")
-        seed = keep.tile([P, 1], F32, name="seed")
-        seed2 = keep.tile([P, 1], F32, name="seed2")
-        pos = keep.tile([P, 1], F32, name="pos")
-        inv = keep.tile([P, HALF], F32, name="inv")
-        phi = keep.tile([P, 3 * HALF], F32, name="phi")
-        turns = keep.tile([P, 3 * HALF], I32, name="turns")
-        red1 = keep.tile([P, 3 * HALF], F32, name="red1")
-        red2 = keep.tile([P, 3 * HALF], F32, name="red2")
-        shalf = keep.tile([P, 3 * HALF], F32, name="shalf")
-        sq = keep.tile([P, 3 * HALF], F32, name="sq")
-        trig = keep.tile([P, 3, HALF], F32, name="trig")
-        rotb = [keep.tile([P, NBLK], F32, name="rotb%d" % b) for b in range(2)]
+        def zero_planes(planes):
+            for t in planes:
+                nc.vector.memset(t[:].bitcast(I32), 0)
 
-        nc.gpsimd.memset(ones[:], 1.0)
-        nc.gpsimd.memset(seed[:], 0.0)
-        nc.gpsimd.iota(pos[:], pattern=[[0, 1]], base=0, channel_multiplier=1, allow_small_or_imprecise_dtypes=True)
-        nc.gpsimd.memset(inv[:, 0:1], 1.0)
-        ratio = ROPE_BASE ** (-1.0 / HALF)
-        for k in range(7):
-            w = 1 << k
-            nc.gpsimd.tensor_scalar(
-                out=inv[:, w : 2 * w], in0=inv[:, 0:w], scalar1=ratio**w, scalar2=0.0, op0=ALU.mult, op1=ALU.add
-            )
-        for i, shift in enumerate((0.0, 0.5 * math.pi, -0.5 * math.pi)):
-            nc.gpsimd.tensor_scalar(
-                out=phi[:, HALF * i : HALF * (i + 1)], in0=inv[:], scalar1=pos[:, 0:1], scalar2=shift, op0=ALU.mult, op1=ALU.add
-            )
-
-        nc.vector.memset(brow[:].bitcast(I32), 0)
-        nc.vector.memset(xs[0][:].bitcast(I32), 0)
-        nc.vector.memset(ws[0][0][:].bitcast(I32), 0)
-        nc.vector.memset(xs[1][:].bitcast(I32), 0)
-        nc.vector.memset(ws[0][1][:].bitcast(I32), 0)
-        nc.vector.memset(ws[1][0][:].bitcast(I32), 0)
-        nc.vector.memset(ws[2][0][:].bitcast(I32), 0)
-
-        nc.scalar.dma_start(out=brow[0:1, :], in_=bias.rearrange("(o n) -> o n", o=1))
-        nc.scalar.activation(out=seed2[:], in_=seed[:], func=FN.Sin)
-
-        def load_codes(t, words, g0, n, c0, c1):
+        def load_codes(t, words, load, byte0, byte1):
+            first, n = load
             nc.sync.dma_start(
                 out=t[:].bitcast(I32),
-                in_=words[g0 : g0 + n, :, c0:c1].rearrange("g p n -> p g n").bitcast(I32),
+                in_=words[first : first + n, :, byte0:byte1].rearrange("g p n -> p g n").bitcast(I32),
             )
 
-        def load_scales(t, scales, g0, n, c0, c1):
-            for q in range(4):
+        def load_scales(t, scales, load, col0, col1):
+            first, n = load
+            for quad in range(4):
                 nc.sync.dma_start(
-                    out=t[32 * q : 32 * q + 4, :, :].bitcast(I32),
-                    in_=scales[g0 : g0 + n, 4 * q : 4 * q + 4, c0:c1].rearrange("g r n -> r g n").bitcast(I32),
+                    out=t[32 * quad : 32 * quad + 4, :, :].bitcast(I32),
+                    in_=scales[first : first + n, 4 * quad : 4 * quad + 4, col0:col1]
+                    .rearrange("g r n -> r g n")
+                    .bitcast(I32),
                 )
 
         def load_x_codes(i):
-            load_codes(xc[i], x_words, x_code_runs[i][0], x_code_runs[i][1], 0, 1024)
-
-        def load_w_codes(b, i):
-            load_codes(wc[b][i], w_words, wc_runs[b][i][0], wc_runs[b][i][1], 1024 * b, 1024 * (b + 1))
+            load_codes(x_codes[i], x_words, EARLY_CODE_LOADS[i], 0, 2 * BATCHES * P)
 
         def load_x_scales(i):
-            load_scales(xs[i], x_scales, first_scale_runs[i][0], first_scale_runs[i][1], 0, 512)
+            load_scales(x_planes[i], x_scales, EARLY_SCALE_LOADS[i], 0, BATCHES * P)
+
+        def load_w_codes(b, i):
+            load_codes(w_codes[b][i], w_words, w_code_loads[b][i], 2 * BLOCK * b, 2 * BLOCK * (b + 1))
 
         def load_w_scales(b, i):
-            load_scales(ws[b][i], w_scales, ws_runs[b][i][0], ws_runs[b][i][1], NBLK * b, NBLK * (b + 1))
+            load_scales(w_planes[b][i], w_scales, w_scale_loads[b][i], BLOCK * b, BLOCK * (b + 1))
 
+        bias_row = keep.tile([P, 3 * BLOCK], BF16, name="bias_row")
+        nc.vector.memset(bias_row[:].bitcast(I32), 0)
+        zero_planes(x_planes[0:1])
+        zero_planes(w_planes[Q_BLOCK][0:1])
+        zero_planes(x_planes[1:2])
+        zero_planes(w_planes[Q_BLOCK][1:2])
+        zero_planes(w_planes[K_BLOCK])
+        zero_planes(w_planes[V_BLOCK])
+
+        nc.scalar.dma_start(out=bias_row[0:1, :], in_=bias.rearrange("(o n) -> o n", o=1))
         load_x_codes(0)
-        load_w_codes(0, 0)
+        load_w_codes(Q_BLOCK, 0)
         load_x_scales(0)
-        load_w_scales(0, 0)
+        load_w_scales(Q_BLOCK, 0)
         load_x_codes(1)
-        load_w_codes(0, 1)
+        load_w_codes(Q_BLOCK, 1)
         load_x_scales(1)
-        load_w_scales(0, 1)
-        load_x_codes(2)
-        load_w_codes(0, 2)
-        load_x_codes(3)
-        load_w_codes(0, 3)
-        load_w_scales(1, 0)
-        load_w_codes(1, 0)
-        load_w_codes(1, 1)
-        load_w_scales(2, 0)
-        load_w_codes(2, 0)
-        load_w_codes(2, 1)
+        load_w_scales(Q_BLOCK, 1)
+        for i in (2, 3):
+            load_x_codes(i)
+            load_w_codes(Q_BLOCK, i)
+        for b in (K_BLOCK, V_BLOCK):
+            load_w_scales(b, 0)
+            load_w_codes(b, 0)
+            load_w_codes(b, 1)
 
-        warm = psum.tile([P, NBLK], F32, name="warm", tag="acc")
-        for i in range(NDUMMY):
-            nc.tensor.matmul(out=warm[:, 0:P], lhsT=ones[:], rhs=ones[:], start=True, stop=True)
-        bp = []
+        ones = keep.tile([P, P], BF16, name="ones")
+        nc.gpsimd.memset(ones[:], 1.0)
+        bias_psum = []
         for b in range(3):
-            bpt = psum.tile([P, NBLK], F32, name="bp%d" % b, tag="acc")
-            nc.tensor.matmul(out=bpt[:], lhsT=ones[:], rhs=brow[:, NBLK * b : NBLK * (b + 1)], start=True, stop=True)
-            bp.append(bpt)
-        for i in range(NBRIDGE):
-            nc.tensor.matmul(out=warm[:], lhsT=ones[:], rhs=brow[:, 0:NBLK], start=True, stop=True)
-
-        nc.vector.tensor_scalar(out=turns[:], in0=phi[:], scalar1=1.0 / (2.0 * math.pi), scalar2=None, op0=ALU.mult)
-        nc.vector.scalar_tensor_tensor(out=red1[:], in0=turns[:], scalar=-TWO_PI_HI, in1=phi[:], op0=ALU.mult, op1=ALU.add)
-        nc.vector.scalar_tensor_tensor(out=red2[:], in0=turns[:], scalar=-TWO_PI_LO, in1=red1[:], op0=ALU.mult, op1=ALU.add)
-        nc.scalar.activation(out=shalf[:], in_=red2[:], func=FN.Sin, scale=0.5)
-        nc.scalar.activation(out=sq[:], in_=shalf[:], func=FN.Square)
-        nc.scalar.activation(out=trig[:].rearrange("p a j -> p (a j)"), in_=sq[:], func=FN.Copy, scale=-2.0, bias=1.0)
-        nc.scalar.copy(out=bias_v[:], in_=bp[2][:])
-
-        cos_b = trig[:, 0:1, :].to_broadcast([P, 4, HALF])
-        sin_b = trig[:, 1:3, :].unsqueeze(1).to_broadcast([P, 2, 2, HALF])
-
-        def rotate_products(src):
-            pc = work.tile([P, NBLK], F32, name="pc")
-            nc.vector.tensor_tensor(
-                out=pc[:].rearrange("p (a j) -> p a j", a=4), in0=src.rearrange("p (a j) -> p a j", a=4), in1=cos_b, op=ALU.mult
+            spread = psum.tile([P, BLOCK], F32, name="spread%d" % b, tag="bank")
+            nc.tensor.matmul(
+                out=spread[:], lhsT=ones[:], rhs=bias_row[:, BLOCK * b : BLOCK * (b + 1)], start=True, stop=True
             )
-            qs = work.tile([P, NBLK], F32, name="qs")
+            bias_psum.append(spread)
+
+        position = keep.tile([P, 1], F32, name="position")
+        nc.gpsimd.iota(position[:], pattern=[[0, 1]], base=0, channel_multiplier=1, allow_small_or_imprecise_dtypes=True)
+        freq = keep.tile([P, HALF], F32, name="freq")
+        nc.gpsimd.memset(freq[:, 0:1], 1.0)
+        ratio = ROPE_BASE ** (-1.0 / HALF)
+        for doubling in range(7):
+            w = 1 << doubling
+            nc.gpsimd.tensor_scalar(
+                out=freq[:, w : 2 * w], in0=freq[:, 0:w], scalar1=ratio**w, scalar2=0.0, op0=ALU.mult, op1=ALU.add
+            )
+        angle = keep.tile([P, 3 * HALF], F32, name="angle")
+        for i, shift in enumerate((0.0, 0.5 * math.pi, -0.5 * math.pi)):
+            nc.gpsimd.tensor_scalar(
+                out=angle[:, HALF * i : HALF * (i + 1)],
+                in0=freq[:],
+                scalar1=position[:, 0:1],
+                scalar2=shift,
+                op0=ALU.mult,
+                op1=ALU.add,
+            )
+        turns = keep.tile([P, 3 * HALF], I32, name="turns")
+        nc.vector.tensor_scalar(out=turns[:], in0=angle[:], scalar1=1.0 / (2.0 * math.pi), scalar2=None, op0=ALU.mult)
+        part = keep.tile([P, 3 * HALF], F32, name="part")
+        nc.vector.scalar_tensor_tensor(
+            out=part[:], in0=turns[:], scalar=-TWO_PI_HI, in1=angle[:], op0=ALU.mult, op1=ALU.add
+        )
+        rest = keep.tile([P, 3 * HALF], F32, name="rest")
+        nc.vector.scalar_tensor_tensor(
+            out=rest[:], in0=turns[:], scalar=-TWO_PI_LO, in1=part[:], op0=ALU.mult, op1=ALU.add
+        )
+        half_sin = keep.tile([P, 3 * HALF], F32, name="half_sin")
+        nc.scalar.activation(out=half_sin[:], in_=rest[:], func=FN.Sin, scale=0.5)
+        half_sin_sq = keep.tile([P, 3 * HALF], F32, name="half_sin_sq")
+        nc.scalar.activation(out=half_sin_sq[:], in_=half_sin[:], func=FN.Square)
+        trig = keep.tile([P, 3, HALF], F32, name="trig")
+        nc.scalar.activation(
+            out=trig[:].rearrange("p a j -> p (a j)"), in_=half_sin_sq[:], func=FN.Copy, scale=-2.0, bias=1.0
+        )
+        bias_v = keep.tile([P, BLOCK], F32, name="bias_v")
+        nc.scalar.copy(out=bias_v[:], in_=bias_psum[V_BLOCK][:])
+
+        cos_table = trig[:, 0:1, :].to_broadcast([P, 2 * HEADS, HALF])
+        sin_table = trig[:, 1:3, :].unsqueeze(1).to_broadcast([P, HEADS, 2, HALF])
+
+        def times_cos(bank):
+            prod = work.tile([P, BLOCK], F32, name="cos_part")
             nc.vector.tensor_tensor(
-                out=qs[:].rearrange("p (h s j) -> p h s j", h=2, s=2),
-                in0=src.rearrange("p (h s j) -> p h s j", h=2, s=2)[:, :, ::-1, :],
-                in1=sin_b,
+                out=prod[:].rearrange("p (a j) -> p a j", j=HALF),
+                in0=bank.rearrange("p (a j) -> p a j", j=HALF),
+                in1=cos_table,
                 op=ALU.mult,
             )
-            return pc, qs
+            return prod
 
-        for b in range(2):
-            pc, qs = rotate_products(bp[b][:])
-            nc.gpsimd.tensor_tensor(out=rotb[b][:], in0=pc[:], in1=qs[:], op=ALU.add)
+        def swapped_times_sin(bank):
+            prod = work.tile([P, BLOCK], F32, name="sin_part")
+            nc.vector.tensor_tensor(
+                out=prod[:].rearrange("p (h s j) -> p h s j", s=2, j=HALF),
+                in0=bank.rearrange("p (h s j) -> p h s j", s=2, j=HALF)[:, :, ::-1, :],
+                in1=sin_table,
+                op=ALU.mult,
+            )
+            return prod
 
-        def mx_pass(acc, t, b, g, c0, c1):
-            xct, xi = find(x_code_runs, xc, g)
-            xst, xj = find(first_scale_runs, xs, g)
-            wct, wi = find(wc_runs[b], wc[b], g)
-            wst, wj = find(ws_runs[b], ws[b], g)
+        rotated_bias = []
+        for b in (Q_BLOCK, K_BLOCK):
+            cos_part = times_cos(bias_psum[b][:])
+            sin_part = swapped_times_sin(bias_psum[b][:])
+            rb = keep.tile([P, BLOCK], F32, name="rotated_bias%d" % b)
+            nc.gpsimd.tensor_tensor(out=rb[:], in0=cos_part[:], in1=sin_part[:], op=ALU.add)
+            rotated_bias.append(rb)
+
+        def mx_pass(bank, batch, b, g, col0, col1):
             nc.tensor.matmul_mx(
-                out=acc[:],
-                lhsT=xct[:, xi, 256 * t : 256 * (t + 1)].bitcast(FP4X4),
-                lhsT_scale=xst[:, xj, P * t : P * (t + 1)],
-                rhs=wct[:, wi, 2 * c0 : 2 * c1].bitcast(FP4X4),
-                rhs_scale=wst[:, wj, c0:c1],
+                out=bank[:],
+                lhsT=of_pass(EARLY_CODE_LOADS, x_codes, g)[:, 2 * P * batch : 2 * P * (batch + 1)].bitcast(FP4X4),
+                lhsT_scale=of_pass(EARLY_SCALE_LOADS, x_planes, g)[:, P * batch : P * (batch + 1)],
+                rhs=of_pass(w_code_loads[b], w_codes[b], g)[:, 2 * col0 : 2 * col1].bitcast(FP4X4),
+                rhs_scale=of_pass(w_scale_loads[b], w_planes[b], g)[:, col0:col1],
                 start=(g == 0),
                 stop=(g == PASSES - 1),
             )
 
-        pending = []
+        waiting = []
 
-        def finish_pending():
-            for (b, t, pc, qs) in pending:
-                nc.vector.tensor_tensor(out=pc[:], in0=pc[:], in1=qs[:], op=ALU.add)
-                res = work.tile([P, NBLK], F32, name="res")
-                nc.gpsimd.tensor_tensor(out=res[:], in0=pc[:], in1=rotb[b][:], op=ALU.add)
-                nc.sync.dma_start(out=outs[b][t].rearrange("h l d -> l h d"), in_=res[:].rearrange("p (h d) -> p h d", h=2))
-            pending.clear()
+        def finish_waiting():
+            for b, batch, cos_part, sin_part in waiting:
+                nc.vector.tensor_tensor(out=cos_part[:], in0=cos_part[:], in1=sin_part[:], op=ALU.add)
+                rotated = work.tile([P, BLOCK], F32, name="rotated")
+                nc.gpsimd.tensor_tensor(out=rotated[:], in0=cos_part[:], in1=rotated_bias[b][:], op=ALU.add)
+                nc.sync.dma_start(
+                    out=outs[b][batch].rearrange("h l d -> l h d"),
+                    in_=rotated[:].rearrange("p (h d) -> p h d", h=HEADS),
+                )
+            waiting.clear()
 
-        def rope_epilogue(acc, b, t):
-            src = acc[:]
-            pc = work.tile([P, NBLK], F32, name="pc")
-            nc.vector.tensor_tensor(
-                out=pc[:].rearrange("p (a j) -> p a j", a=4), in0=src.rearrange("p (a j) -> p a j", a=4), in1=cos_b, op=ALU.mult
-            )
-            finish_pending()
-            qs = work.tile([P, NBLK], F32, name="qs")
-            nc.vector.tensor_tensor(
-                out=qs[:].rearrange("p (h s j) -> p h s j", h=2, s=2),
-                in0=src.rearrange("p (h s j) -> p h s j", h=2, s=2)[:, :, ::-1, :],
-                in1=sin_b,
-                op=ALU.mult,
-            )
-            pending.append((b, t, pc, qs))
+        def rotate(bank, b, batch):
+            cos_part = times_cos(bank[:])
+            finish_waiting()
+            sin_part = swapped_times_sin(bank[:])
+            waiting.append((b, batch, cos_part, sin_part))
 
-        accs = []
-        for t in range(TILES):
-            acc = psum.tile([P, NBLK], F32, name="acc", tag="acc")
-            accs.append(acc)
-        for g in range(SPLIT_Q):
-            for t in range(TILES):
-                mx_pass(accs[t], t, 0, g, 0, NBLK)
-        for t in range(TILES):
-            for g in range(SPLIT_Q, PASSES):
-                mx_pass(accs[t], t, 0, g, 0, NBLK)
-            rope_epilogue(accs[t], 0, t)
-        accs = []
-        for t in range(TILES):
-            acc = psum.tile([P, NBLK], F32, name="acc", tag="acc")
-            accs.append(acc)
-        for g in range(SPLIT_K):
-            for t in range(TILES):
-                mx_pass(accs[t], t, 1, g, 0, NBLK)
-        for t in range(TILES):
-            for g in range(SPLIT_K, PASSES):
-                mx_pass(accs[t], t, 1, g, 0, NBLK)
-            rope_epilogue(accs[t], 1, t)
-        for t in range(TILES - 1):
-            acc = psum.tile([P, NBLK], F32, name="acc", tag="acc")
+        for b in (Q_BLOCK, K_BLOCK):
+            banks = [psum.tile([P, BLOCK], F32, name="bank%d" % batch, tag="bank") for batch in range(BATCHES)]
+            for g in range(PASS_OUTER[b]):
+                for batch in range(BATCHES):
+                    mx_pass(banks[batch], batch, b, g, 0, BLOCK)
+            for batch in range(BATCHES):
+                for g in range(PASS_OUTER[b], PASSES):
+                    mx_pass(banks[batch], batch, b, g, 0, BLOCK)
+                rotate(banks[batch], b, batch)
+
+        for batch in range(BATCHES - 1):
+            bank = psum.tile([P, BLOCK], F32, name="bank_v", tag="bank")
             for g in range(PASSES):
-                mx_pass(acc, t, 2, g, 0, NBLK)
-            resv = work.tile([P, NBLK], F32, name="resv")
-            nc.vector.tensor_tensor(out=resv[:], in0=acc[:], in1=bias_v[:], op=ALU.add)
-            finish_pending()
-            nc.scalar.dma_start(out=out_v[t].rearrange("h l d -> l h d"), in_=resv[:].rearrange("p (h d) -> p h d", h=2))
-        t = TILES - 1
-        for h in range(2):
-            acc = psum.tile([P, NBLK // 2], F32, name="acch", tag="acc")
+                mx_pass(bank, batch, V_BLOCK, g, 0, BLOCK)
+            v_out = work.tile([P, BLOCK], F32, name="v_out")
+            nc.vector.tensor_tensor(out=v_out[:], in0=bank[:], in1=bias_v[:], op=ALU.add)
+            finish_waiting()
+            nc.scalar.dma_start(
+                out=out_v[batch].rearrange("h l d -> l h d"), in_=v_out[:].rearrange("p (h d) -> p h d", h=HEADS)
+            )
+        head_width = BLOCK // HEADS
+        for h, queue in enumerate((nc.scalar, nc.sync)):
+            bank = psum.tile([P, head_width], F32, name="bank_head", tag="bank")
             for g in range(PASSES):
-                mx_pass(acc, t, 2, g, 256 * h, 256 * (h + 1))
-            resh = work.tile([P, NBLK // 2], F32, name="resh")
-            nc.vector.tensor_tensor(out=resh[:], in0=acc[:], in1=bias_v[:, 256 * h : 256 * (h + 1)], op=ALU.add)
-            eng = nc.scalar if h == 0 else nc.sync
-            eng.dma_start(out=out_v[t][h], in_=resh[:])
+                mx_pass(bank, BATCHES - 1, V_BLOCK, g, head_width * h, head_width * (h + 1))
+            head_out = work.tile([P, head_width], F32, name="head_out")
+            nc.vector.tensor_tensor(
+                out=head_out[:], in0=bank[:], in1=bias_v[:, head_width * h : head_width * (h + 1)], op=ALU.add
+            )
+            queue.dma_start(out=out_v[BATCHES - 1][h], in_=head_out[:])

from contextlib import ExitStack
import math

import concourse.mybir as mybir

FLOPS = 2 * 512 * 4096 * 1536

F32 = mybir.dt.float32
BF16 = mybir.dt.bfloat16
I32 = mybir.dt.int32
U8 = mybir.dt.uint8
FP4X4 = mybir.dt.float4_e2m1fn_x4
ALU = mybir.AluOpType
FN = mybir.ActivationFunctionType

P = 128
PASSES = 8
BATCHES = 4
BLOCK = 512
HEADS = 2
HALF = 128
ROPE_BASE = 10000.0
Q_BLOCK = 0
K_BLOCK = 1
V_BLOCK = 2

TWO_PI_HI = 6.28125
TWO_PI_LO = 2.0 * math.pi - TWO_PI_HI

EARLY_CODE_LOADS = [(0, 1), (1, 3), (4, 2), (6, 2)]
LATE_CODE_LOADS = [(0, 4), (4, 4)]
EARLY_SCALE_LOADS = [(0, 4), (4, 4)]
LATE_SCALE_LOADS = [(0, 8)]

PASS_OUTER = {Q_BLOCK: 8, K_BLOCK: 4}


def tile_ropeattention_pa_kernel(tc, x_words, x_scales, w_words, w_scales, bias, out_q, out_k, out_v):
    nc = tc.nc
    outs = [out_q, out_k, out_v]

    with ExitStack() as ctx:
        keep = ctx.enter_context(tc.tile_pool(name="keep", bufs=1))
        work = ctx.enter_context(tc.tile_pool(name="work", bufs=4))
        psum = ctx.enter_context(tc.psum_pool(name="psum", bufs=8))
        ctx.enter_context(tc.manual_schedule())

        def byte_tiles(name, loads, row_bytes):
            return [
                keep.tile([P, n, row_bytes], U8, name="%s_%d" % (name, i), align_bytes=64)
                for i, (first, n) in enumerate(loads)
            ]

        w_code_loads = [EARLY_CODE_LOADS, LATE_CODE_LOADS, LATE_CODE_LOADS]
        w_scale_loads = [EARLY_SCALE_LOADS, LATE_SCALE_LOADS, LATE_SCALE_LOADS]
        x_codes = byte_tiles("x_codes", EARLY_CODE_LOADS, 2 * BATCHES * P)
        x_planes = byte_tiles("x_planes", EARLY_SCALE_LOADS, BATCHES * P)
        w_codes = [byte_tiles("w_codes%d" % b, w_code_loads[b], 2 * BLOCK) for b in range(3)]
        w_planes = [byte_tiles("w_planes%d" % b, w_scale_loads[b], BLOCK) for b in range(3)]

        def of_pass(loads, tiles, g):
            for (first, n), t in zip(loads, tiles):
                if first <= g < first + n:
                    return t[:, g - first, :]
            raise ValueError("pass not loaded")

        def zero_planes(planes):
            for t in planes:
                nc.vector.memset(t[:].bitcast(I32), 0)

        def load_codes(t, words, load, byte0, byte1):
            first, n = load
            nc.sync.dma_start(
                out=t[:].bitcast(I32),
                in_=words[first : first + n, :, byte0:byte1].rearrange("g p n -> p g n").bitcast(I32),
            )

        def load_scales(t, scales, load, col0, col1):
            first, n = load
            for quad in range(4):
                nc.sync.dma_start(
                    out=t[32 * quad : 32 * quad + 4, :, :].bitcast(I32),
                    in_=scales[first : first + n, 4 * quad : 4 * quad + 4, col0:col1]
                    .rearrange("g r n -> r g n")
                    .bitcast(I32),
                )

        def load_x_codes(i):
            load_codes(x_codes[i], x_words, EARLY_CODE_LOADS[i], 0, 2 * BATCHES * P)

        def load_x_scales(i):
            load_scales(x_planes[i], x_scales, EARLY_SCALE_LOADS[i], 0, BATCHES * P)

        def load_w_codes(b, i):
            load_codes(w_codes[b][i], w_words, w_code_loads[b][i], 2 * BLOCK * b, 2 * BLOCK * (b + 1))

        def load_w_scales(b, i):
            load_scales(w_planes[b][i], w_scales, w_scale_loads[b][i], BLOCK * b, BLOCK * (b + 1))

        bias_row = keep.tile([P, 3 * BLOCK], BF16, name="bias_row")
        nc.vector.memset(bias_row[:].bitcast(I32), 0)
        zero_planes(x_planes[0:1])
        zero_planes(w_planes[Q_BLOCK][0:1])
        zero_planes(x_planes[1:2])
        zero_planes(w_planes[Q_BLOCK][1:2])
        zero_planes(w_planes[K_BLOCK])
        zero_planes(w_planes[V_BLOCK])

        nc.scalar.dma_start(out=bias_row[0:1, :], in_=bias.rearrange("(o n) -> o n", o=1))
        load_x_codes(0)
        load_w_codes(Q_BLOCK, 0)
        load_x_scales(0)
        load_w_scales(Q_BLOCK, 0)
        load_x_codes(1)
        load_w_codes(Q_BLOCK, 1)
        load_x_scales(1)
        load_w_scales(Q_BLOCK, 1)
        for i in (2, 3):
            load_x_codes(i)
            load_w_codes(Q_BLOCK, i)
        for b in (K_BLOCK, V_BLOCK):
            load_w_scales(b, 0)
            load_w_codes(b, 0)
            load_w_codes(b, 1)

        ones = keep.tile([P, P], BF16, name="ones")
        nc.gpsimd.memset(ones[:], 1.0)
        bias_psum = []
        for b in range(3):
            spread = psum.tile([P, BLOCK], F32, name="spread%d" % b, tag="bank")
            nc.tensor.matmul(
                out=spread[:], lhsT=ones[:], rhs=bias_row[:, BLOCK * b : BLOCK * (b + 1)], start=True, stop=True
            )
            bias_psum.append(spread)

        position = keep.tile([P, 1], F32, name="position")
        nc.gpsimd.iota(position[:], pattern=[[0, 1]], base=0, channel_multiplier=1, allow_small_or_imprecise_dtypes=True)
        freq = keep.tile([P, HALF], F32, name="freq")
        nc.gpsimd.memset(freq[:, 0:1], 1.0)
        ratio = ROPE_BASE ** (-1.0 / HALF)
        for doubling in range(7):
            w = 1 << doubling
            nc.gpsimd.tensor_scalar(
                out=freq[:, w : 2 * w], in0=freq[:, 0:w], scalar1=ratio**w, scalar2=0.0, op0=ALU.mult, op1=ALU.add
            )
        angle = keep.tile([P, 3 * HALF], F32, name="angle")
        for i, shift in enumerate((0.0, 0.5 * math.pi, -0.5 * math.pi)):
            nc.gpsimd.tensor_scalar(
                out=angle[:, HALF * i : HALF * (i + 1)],
                in0=freq[:],
                scalar1=position[:, 0:1],
                scalar2=shift,
                op0=ALU.mult,
                op1=ALU.add,
            )
        turns = keep.tile([P, 3 * HALF], I32, name="turns")
        nc.vector.tensor_scalar(out=turns[:], in0=angle[:], scalar1=1.0 / (2.0 * math.pi), scalar2=None, op0=ALU.mult)
        part = keep.tile([P, 3 * HALF], F32, name="part")
        nc.vector.scalar_tensor_tensor(
            out=part[:], in0=turns[:], scalar=-TWO_PI_HI, in1=angle[:], op0=ALU.mult, op1=ALU.add
        )
        rest = keep.tile([P, 3 * HALF], F32, name="rest")
        nc.vector.scalar_tensor_tensor(
            out=rest[:], in0=turns[:], scalar=-TWO_PI_LO, in1=part[:], op0=ALU.mult, op1=ALU.add
        )
        half_sin = keep.tile([P, 3 * HALF], F32, name="half_sin")
        nc.scalar.activation(out=half_sin[:], in_=rest[:], func=FN.Sin, scale=0.5)
        half_sin_sq = keep.tile([P, 3 * HALF], F32, name="half_sin_sq")
        nc.scalar.activation(out=half_sin_sq[:], in_=half_sin[:], func=FN.Square)
        trig = keep.tile([P, 3, HALF], F32, name="trig")
        nc.scalar.activation(
            out=trig[:].rearrange("p a j -> p (a j)"), in_=half_sin_sq[:], func=FN.Copy, scale=-2.0, bias=1.0
        )
        bias_v = keep.tile([P, BLOCK], F32, name="bias_v")
        nc.scalar.copy(out=bias_v[:], in_=bias_psum[V_BLOCK][:])

        cos_table = trig[:, 0:1, :].to_broadcast([P, 2 * HEADS, HALF])
        sin_table = trig[:, 1:3, :].unsqueeze(1).to_broadcast([P, HEADS, 2, HALF])

        def times_cos(bank):
            prod = work.tile([P, BLOCK], F32, name="cos_part")
            nc.vector.tensor_tensor(
                out=prod[:].rearrange("p (a j) -> p a j", j=HALF),
                in0=bank.rearrange("p (a j) -> p a j", j=HALF),
                in1=cos_table,
                op=ALU.mult,
            )
            return prod

        def swapped_times_sin(bank):
            prod = work.tile([P, BLOCK], F32, name="sin_part")
            nc.vector.tensor_tensor(
                out=prod[:].rearrange("p (h s j) -> p h s j", s=2, j=HALF),
                in0=bank.rearrange("p (h s j) -> p h s j", s=2, j=HALF)[:, :, ::-1, :],
                in1=sin_table,
                op=ALU.mult,
            )
            return prod

        rotated_bias = []
        for b in (Q_BLOCK, K_BLOCK):
            cos_part = times_cos(bias_psum[b][:])
            sin_part = swapped_times_sin(bias_psum[b][:])
            rb = keep.tile([P, BLOCK], F32, name="rotated_bias%d" % b)
            nc.gpsimd.tensor_tensor(out=rb[:], in0=cos_part[:], in1=sin_part[:], op=ALU.add)
            rotated_bias.append(rb)

        def mx_pass(bank, batch, b, g, col0, col1):
            nc.tensor.matmul_mx(
                out=bank[:],
                lhsT=of_pass(EARLY_CODE_LOADS, x_codes, g)[:, 2 * P * batch : 2 * P * (batch + 1)].bitcast(FP4X4),
                lhsT_scale=of_pass(EARLY_SCALE_LOADS, x_planes, g)[:, P * batch : P * (batch + 1)],
                rhs=of_pass(w_code_loads[b], w_codes[b], g)[:, 2 * col0 : 2 * col1].bitcast(FP4X4),
                rhs_scale=of_pass(w_scale_loads[b], w_planes[b], g)[:, col0:col1],
                start=(g == 0),
                stop=(g == PASSES - 1),
            )

        waiting = []

        def finish_waiting():
            for b, batch, cos_part, sin_part in waiting:
                nc.vector.tensor_tensor(out=cos_part[:], in0=cos_part[:], in1=sin_part[:], op=ALU.add)
                rotated = work.tile([P, BLOCK], F32, name="rotated")
                nc.gpsimd.tensor_tensor(out=rotated[:], in0=cos_part[:], in1=rotated_bias[b][:], op=ALU.add)
                nc.sync.dma_start(
                    out=outs[b][batch].rearrange("h l d -> l h d"),
                    in_=rotated[:].rearrange("p (h d) -> p h d", h=HEADS),
                )
            waiting.clear()

        def rotate(bank, b, batch):
            cos_part = times_cos(bank[:])
            finish_waiting()
            sin_part = swapped_times_sin(bank[:])
            waiting.append((b, batch, cos_part, sin_part))

        for b in (Q_BLOCK, K_BLOCK):
            banks = [psum.tile([P, BLOCK], F32, name="bank%d" % batch, tag="bank") for batch in range(BATCHES)]
            for g in range(PASS_OUTER[b]):
                for batch in range(BATCHES):
                    mx_pass(banks[batch], batch, b, g, 0, BLOCK)
            for batch in range(BATCHES):
                for g in range(PASS_OUTER[b], PASSES):
                    mx_pass(banks[batch], batch, b, g, 0, BLOCK)
                rotate(banks[batch], b, batch)

        for batch in range(BATCHES - 1):
            bank = psum.tile([P, BLOCK], F32, name="bank_v", tag="bank")
            for g in range(PASSES):
                mx_pass(bank, batch, V_BLOCK, g, 0, BLOCK)
            v_out = work.tile([P, BLOCK], F32, name="v_out")
            nc.vector.tensor_tensor(out=v_out[:], in0=bank[:], in1=bias_v[:], op=ALU.add)
            finish_waiting()
            nc.scalar.dma_start(
                out=out_v[batch].rearrange("h l d -> l h d"), in_=v_out[:].rearrange("p (h d) -> p h d", h=HEADS)
            )
        head_width = BLOCK // HEADS
        for h, queue in enumerate((nc.scalar, nc.sync)):
            bank = psum.tile([P, head_width], F32, name="bank_head", tag="bank")
            for g in range(PASSES):
                mx_pass(bank, BATCHES - 1, V_BLOCK, g, head_width * h, head_width * (h + 1))
            head_out = work.tile([P, head_width], F32, name="head_out")
            nc.vector.tensor_tensor(
                out=head_out[:], in0=bank[:], in1=bias_v[:, head_width * h : head_width * (h + 1)], op=ALU.add
            )
            queue.dma_start(out=out_v[BATCHES - 1][h], in_=head_out[:])
